import numpy as np
import ml_dtypes


def mxq(x, axis, fmt="e4m3"):
    dtype, down = {"e4m3": (ml_dtypes.float8_e4m3fn, 7), "e5m2": (ml_dtypes.float8_e5m2, 14)}[fmt]
    v = np.moveaxis(np.asarray(x, np.float32).astype(ml_dtypes.bfloat16).astype(np.float64), axis, -1)
    blocks = v.reshape(v.shape[:-1] + (-1, 32))
    amax = np.abs(blocks).max(-1, keepdims=True)
    byte = np.maximum(np.where(amax > 0, np.frexp(amax)[1] - 1 + 127, 0) - down, 1)
    scale = np.exp2(byte - 127.0)
    codes = (blocks / scale).astype(np.float32).astype(dtype).astype(np.float64)
    return np.moveaxis((codes * scale).reshape(v.shape), -1, axis)


WIDE = False


def mx_kscale(k):
    if not WIDE:
        return np.ones(k)
    levels = np.array([10, -10, 5, -5, 0])
    a = np.random.permutation(np.resize(levels, k // 512 * 4)).reshape(k // 512, 4)
    idx = np.arange(k)
    return np.exp2(a[idx // 512, idx % 128 // 32])


BF16 = ml_dtypes.bfloat16


def bf(x):
    return np.asarray(x, np.float32).astype(BF16)


def f64(x):
    return np.asarray(x).astype(np.float64)


B, S, L, C, K0, K1, K2, NC = 4, 8, 8192, 4, 512, 512, 16, 10
T = S * L
R = B * S


def setup_inputs():
    t = mx_kscale(K0)
    level = np.random.standard_normal((B, S, C))
    x = np.random.standard_normal((B, S, L, C)) + 0.5 * level[:, :, None, :]
    return {"x": bf(x.reshape(B, T, C)),
            "W0": bf(np.random.standard_normal((C, L, K0)) / np.sqrt(L) * t),
            "b0": bf(np.random.standard_normal((C, K0)) * 0.3 * t),
            "W1": bf(np.random.standard_normal((C, K0, K1)) * 1.4 / np.sqrt(K0) / t[:, None]),
            "b1": bf(np.random.standard_normal((C, K1)) * 0.3)}


def reference(x, W0, b0, W1, b1):
    xc = f64(x).reshape(B, S, L, C)
    mid = (xc.min(axis=2) + xc.max(axis=2)) * 0.5
    norm = xc - mid[:, :, None, :]
    nt = norm.transpose(3, 0, 1, 2).reshape(C, R, L)
    h0 = np.maximum((mxq(nt, 2, "e4m3") @ mxq(f64(W0), 1, "e4m3")) + f64(b0)[:, None, :], 0.0)
    h1 = np.maximum((mxq(h0, 2, "e4m3") @ mxq(f64(W1), 1, "e4m3")) + f64(b1)[:, None, :], 0.0)
    return h1.reshape(C, B, S, K1).transpose(1, 2, 0, 3)

@@ -1,0 +1,225 @@
+from contextlib import ExitStack
+
+import concourse.mybir as mybir
+from concourse.masks import make_identity
+
+FP8X4 = mybir.dt.float8_e4m3fn_x4
+BF16 = mybir.dt.bfloat16
+F32 = mybir.dt.float32
+U32 = mybir.dt.uint32
+U8 = mybir.dt.uint8
+ALU = mybir.AluOpType
+ACT = mybir.ActivationFunctionType
+
+P = 128
+PACK = 4
+B, S, L, C, K0, K1 = 4, 8, 8192, 4, 512, 512
+R = B * S
+PASSES = L // (P * PACK)
+OWN = L // P
+FILTER_TILES = K0 // P
+
+FLOPS = 2 * R * C * (L * K0 + K0 * K1)
+
+W1_PAIRS = C // 2
+PAIRS = W1_PAIRS + C * PASSES // 2
+HEAD_PAIRS = 8
+RAW_BUFS = 10
+GROUPED_BUFS = 12
+CODE_BUFS = 8
+X_ROUND = 4
+
+
+def tile_shapeletencoder_pa_k_kernel(tc, x, W0, b0, W1, b1, out):
+    nc = tc.nc
+    with ExitStack() as ctx:
+        keep = ctx.enter_context(tc.tile_pool(name="keep", bufs=1))
+        raw_pool = ctx.enter_context(tc.tile_pool(name="raw", bufs=RAW_BUFS))
+        grouped_pool = ctx.enter_context(tc.tile_pool(name="grouped", bufs=GROUPED_BUFS))
+        code_pool = ctx.enter_context(tc.tile_pool(name="codes", bufs=CODE_BUFS))
+        psum = ctx.enter_context(tc.psum_pool(name="psum", bufs=1))
+
+        ident_bf16 = keep.tile([P, P], BF16)
+        make_identity(nc, ident_bf16[:])
+        ident_f32 = keep.tile([P, P], F32)
+        make_identity(nc, ident_f32[:])
+        halves = keep.tile([P, P], F32)
+        nc.vector.memset(halves[:], 0.5)
+        b0_rows = keep.tile([P, P], BF16)
+        nc.vector.memset(b0_rows[:], 0.0)
+        h0_grouped = keep.tile([P, C, P, PACK], BF16, align_bytes=64)
+        nc.vector.memset(h0_grouped[:], 0.0)
+
+        x_sb = keep.tile([P, R, OWN * C], BF16)
+        for b in range(B):
+            nc.sync.dma_start(
+                out=x_sb[:, S * b : S * (b + 1), :],
+                in_=x[b].rearrange("(s p f) c -> p s (f c)", s=S, p=P, f=OWN),
+            )
+
+        w0_rows = W0.rearrange("c (p g j) f -> c p g j f", p=P, g=PASSES, j=PACK)
+        w1_rows = W1.rearrange("c (t p) n -> p c t n", p=P)
+
+        def load_pair(i):
+            raw = raw_pool.tile([P, 2, PACK, K0], BF16, name="raw")
+            if i < W1_PAIRS:
+                rows = w1_rows[:, 2 * i : 2 * i + 2]
+            else:
+                c, g = divmod(2 * (i - W1_PAIRS), PASSES)
+                rows = w0_rows[c, :, g : g + 2]
+            nc.sync.dma_start(out=raw[:], in_=rows)
+            return raw
+
+        raws = [load_pair(i) for i in range(RAW_BUFS)]
+
+        nc.sync.dma_start(out=b0_rows[0 : C * FILTER_TILES, :], in_=b0.rearrange("c (t p) -> (c t) p", p=P))
+        b1_rows = keep.tile([P, K1], BF16)
+        for c in range(C):
+            nc.sync.dma_start(out=b1_rows[c:P:C, :], in_=b1[c].partition_broadcast(R))
+
+        hi = keep.tile([P, R, OWN * C // 2], BF16)
+        lo = keep.tile([P, R, OWN * C // 2], BF16)
+        part_max = keep.tile([P, R * C], BF16)
+        part_min = keep.tile([P, R * C], BF16)
+        width = OWN * C // 2
+        for b in range(B):
+            cells = slice(S * b, S * (b + 1))
+            for extreme, op in ((hi, ALU.max), (lo, ALU.min)):
+                nc.vector.tensor_tensor(
+                    out=extreme[:, cells, :], in0=x_sb[:, cells, :width], in1=x_sb[:, cells, width:], op=op
+                )
+        while width > C:
+            width //= 2
+            for extreme, last, op in ((hi, part_max, ALU.max), (lo, part_min, ALU.min)):
+                nc.vector.tensor_tensor(
+                    out=last[:].rearrange("p (r c) -> p r c", c=C) if width == C else extreme[:, :, :width],
+                    in0=extreme[:, :, :width],
+                    in1=extreme[:, :, width : 2 * width],
+                    op=op,
+                )
+
+        flipped = psum.tile([P, 2, P], BF16, tag="flip")
+        nc.tensor.transpose(flipped[:, 0, :], part_max[:], ident_bf16[:])
+        nc.tensor.transpose(flipped[:, 1, :], part_min[:], ident_bf16[:])
+        ends = keep.tile([P, 2], F32)
+        nc.vector.tensor_reduce(out=ends[:, 0:1], in_=flipped[:, 0, :], axis=mybir.AxisListType.X, op=ALU.max)
+        nc.vector.tensor_reduce(out=ends[:, 1:2], in_=flipped[:, 1, :], axis=mybir.AxisListType.X, op=ALU.min)
+        total = keep.tile([P, 1], F32)
+        nc.vector.tensor_tensor(out=total[:], in0=ends[:, 0:1], in1=ends[:, 1:2], op=ALU.add)
+        mid_repeated = keep.tile([P, P], F32)
+        nc.vector.tensor_scalar(out=mid_repeated[:], in0=halves[:], scalar1=total[:, 0:1], scalar2=None, op0=ALU.mult)
+        mid = psum.tile([P, P], F32)
+        nc.tensor.transpose(mid[:], mid_repeated[:], ident_f32[:])
+        mid_rjc = mid[:].rearrange("p (r c) -> p r c", c=C).unsqueeze(2).to_broadcast([P, R, PACK, C])
+
+        x_codes = keep.tile([P, PASSES, P], U32, align_bytes=64)
+        x_scales = keep.tile([P, PASSES, P], U8, align_bytes=64)
+        x_rounds = PASSES // X_ROUND
+        n_tiles = []
+        for q in range(x_rounds + 1):
+            if q < x_rounds:
+                n_grouped = keep.tile([P, X_ROUND, P * PACK], BF16, bufs=2, align_bytes=64)
+                n_tiles.append(n_grouped)
+                for k in range(X_ROUND):
+                    first = (X_ROUND * q + k) * PACK * C
+                    nc.vector.tensor_tensor(
+                        out=n_grouped[:, k, :].rearrange("p (r c j) -> p r j c", r=R, c=C, j=PACK),
+                        in0=x_sb[:, :, first : first + PACK * C].rearrange("p r (j c) -> p r j c", c=C),
+                        in1=mid_rjc,
+                        op=ALU.subtract,
+                    )
+            if q > 0:
+                done = slice(X_ROUND * (q - 1), X_ROUND * q)
+                nc.vector.quantize_mx(
+                    out=x_codes[:, done, :].rearrange("p g m -> p (g m)").bitcast(FP8X4),
+                    scales=x_scales[:, done, :].rearrange("p g m -> p (g m)"),
+                    in_=n_tiles[q - 1][:].rearrange("p g w -> p (g w)"),
+                )
+
+        b0_flipped = psum.tile([P, P], BF16, tag="flip")
+        nc.tensor.transpose(b0_flipped[:], b0_rows[:], ident_bf16[:])
+        b0_cols = keep.tile([P, C * FILTER_TILES], F32)
+        nc.vector.tensor_copy(out=b0_cols[:], in_=b0_flipped[:, 0 : C * FILTER_TILES])
+
+        w1_codes = keep.tile([P, C, K1], U32, align_bytes=64)
+        w1_scales = keep.tile([P, C, K1], U8, align_bytes=64)
+        h0_codes = keep.tile([P, C, P], U32, align_bytes=64)
+        h0_scales = keep.tile([P, C, P], U8, align_bytes=64)
+        out_acc = psum.tile([P, K1], F32)
+        acc = []
+
+        regrouped = []
+        for i in range(PAIRS + 1):
+            fresh = []
+            if i < PAIRS:
+                for h in range(2):
+                    grouped = grouped_pool.tile([P, K0, PACK], BF16, align_bytes=64)
+                    copy = nc.vector.tensor_copy if (h == 1 and i >= HEAD_PAIRS) else nc.scalar.copy
+                    copy(
+                        out=grouped[:].rearrange("p (w i) t -> p w t i", i=4),
+                        in_=raws[i][:, h].rearrange("p t (w i) -> p w t i", i=4),
+                    )
+                    fresh.append((2 * i + h, grouped))
+                if i + RAW_BUFS < PAIRS:
+                    raws.append(load_pair(i + RAW_BUFS))
+
+            for number, grouped in regrouped:
+                values = grouped[:].rearrange("p w t -> p (w t)")
+                if number < C:
+                    nc.vector.quantize_mx(
+                        out=w1_codes[:, number, :].bitcast(FP8X4), scales=w1_scales[:, number, :], in_=values
+                    )
+                    continue
+
+                c, g = divmod(number - C, PASSES)
+                w0_codes = code_pool.tile([P, K0], U32, align_bytes=64)
+                w0_scales = code_pool.tile([P, K0], U8, align_bytes=64)
+                nc.vector.quantize_mx(out=w0_codes[:].bitcast(FP8X4), scales=w0_scales[:], in_=values)
+                if g == 0:
+                    acc = [psum.tile([P, P], F32, name="acc%d" % t) for t in range(FILTER_TILES)]
+                for t in range(FILTER_TILES):
+                    filters = slice(P * t, P * (t + 1))
+                    nc.tensor.matmul_mx(
+                        out=acc[t][:],
+                        lhsT=w0_codes[:, filters].bitcast(FP8X4),
+                        lhsT_scale=w0_scales[:, filters],
+                        rhs=x_codes[:, g, :].bitcast(FP8X4),
+                        rhs_scale=x_scales[:, g, :],
+                        start=(g == 0),
+                        stop=(g == PASSES - 1),
+                    )
+                if g < PASSES - 1:
+                    continue
+
+                own_columns = h0_grouped[:, c].rearrange("p (r k) t -> p r k t", k=C)
+                for t in range(FILTER_TILES):
+                    nc.scalar.activation(
+                        out=own_columns[:, :, c, t],
+                        in_=acc[t][:].rearrange("p (r k) -> p r k", k=C)[:, :, c],
+                        func=ACT.Relu,
+                        bias=b0_cols[:, FILTER_TILES * c + t : FILTER_TILES * c + t + 1],
+                        scale=1.0,
+                    )
+                nc.vector.quantize_mx(
+                    out=h0_codes[:, c, :].bitcast(FP8X4),
+                    scales=h0_scales[:, c, :],
+                    in_=h0_grouped[:, c].rearrange("p m t -> p (m t)"),
+                )
+                nc.tensor.matmul_mx(
+                    out=out_acc[:],
+                    lhsT=h0_codes[:, c, :].bitcast(FP8X4),
+                    lhsT_scale=h0_scales[:, c, :],
+                    rhs=w1_codes[:, c, :].bitcast(FP8X4),
+                    rhs_scale=w1_scales[:, c, :],
+                    start=(c == 0),
+                    stop=(c == C - 1),
+                )
+            regrouped = fresh
+
+        result = keep.tile([P, K1], F32)
+        out_rows = out.rearrange("b s c k -> (b s c) k")
+        for half in range(2):
+            cols = slice(K1 // 2 * half, K1 // 2 * (half + 1))
+            nc.vector.tensor_tensor(out=result[:, cols], in0=out_acc[:, cols], in1=b1_rows[:, cols], op=ALU.add)
+            nc.scalar.activation(out=result[:, cols], in_=result[:, cols], func=ACT.Relu)
+            nc.sync.dma_start(out=out_rows[:, cols], in_=result[:, cols])

@@ -23,7 +23,7 @@ FLOPS = 2 * R * C * (L * K0 + K0 * K1)
 
 W1_PAIRS = C // 2
 PAIRS = W1_PAIRS + C * PASSES // 2
-HEAD_PAIRS = 8
+HEAD_PAIRS = 5
 RAW_BUFS = 10
 GROUPED_BUFS = 12
 CODE_BUFS = 8
@@ -38,6 +38,7 @@ def tile_shapeletencoder_pa_k_kernel(tc, x, W0, b0, W1, b1, out):
         grouped_pool = ctx.enter_context(tc.tile_pool(name="grouped", bufs=GROUPED_BUFS))
         code_pool = ctx.enter_context(tc.tile_pool(name="codes", bufs=CODE_BUFS))
         psum = ctx.enter_context(tc.psum_pool(name="psum", bufs=1))
+        ctx.enter_context(tc.manual_schedule())
 
         ident_bf16 = keep.tile([P, P], BF16)
         make_identity(nc, ident_bf16[:])
@@ -57,6 +58,8 @@ def tile_shapeletencoder_pa_k_kernel(tc, x, W0, b0, W1, b1, out):
                 in_=x[b].rearrange("(s p f) c -> p s (f c)", s=S, p=P, f=OWN),
             )
 
+        nc.sync.dma_start(out=b0_rows[0 : C * FILTER_TILES, :], in_=b0.rearrange("c (t p) -> (c t) p", p=P))
+
         w0_rows = W0.rearrange("c (p g j) f -> c p g j f", p=P, g=PASSES, j=PACK)
         w1_rows = W1.rearrange("c (t p) n -> p c t n", p=P)
 
@@ -72,7 +75,6 @@ def tile_shapeletencoder_pa_k_kernel(tc, x, W0, b0, W1, b1, out):
 
         raws = [load_pair(i) for i in range(RAW_BUFS)]
 
-        nc.sync.dma_start(out=b0_rows[0 : C * FILTER_TILES, :], in_=b0.rearrange("c (t p) -> (c t) p", p=P))
         b1_rows = keep.tile([P, K1], BF16)
         for c in range(C):
             nc.sync.dma_start(out=b1_rows[c:P:C, :], in_=b1[c].partition_broadcast(R))
@@ -81,22 +83,28 @@ def tile_shapeletencoder_pa_k_kernel(tc, x, W0, b0, W1, b1, out):
         lo = keep.tile([P, R, OWN * C // 2], BF16)
         part_max = keep.tile([P, R * C], BF16)
         part_min = keep.tile([P, R * C], BF16)
-        width = OWN * C // 2
-        for b in range(B):
-            cells = slice(S * b, S * (b + 1))
-            for extreme, op in ((hi, ALU.max), (lo, ALU.min)):
-                nc.vector.tensor_tensor(
-                    out=extreme[:, cells, :], in0=x_sb[:, cells, :width], in1=x_sb[:, cells, width:], op=op
-                )
-        while width > C:
-            width //= 2
-            for extreme, last, op in ((hi, part_max, ALU.max), (lo, part_min, ALU.min)):
-                nc.vector.tensor_tensor(
-                    out=last[:].rearrange("p (r c) -> p r c", c=C) if width == C else extreme[:, :, :width],
-                    in0=extreme[:, :, :width],
-                    in1=extreme[:, :, width : 2 * width],
-                    op=op,
-                )
+        for first_b in range(0, B, 2):
+            width = OWN * C // 2
+            for b in (first_b, first_b + 1):
+                cells = slice(S * b, S * (b + 1))
+                for extreme, op in ((hi, ALU.max), (lo, ALU.min)):
+                    nc.vector.tensor_tensor(
+                        out=extreme[:, cells, :], in0=x_sb[:, cells, :width], in1=x_sb[:, cells, width:], op=op
+                    )
+            cells = slice(S * first_b, S * (first_b + 2))
+            while width > C:
+                width //= 2
+                for extreme, last, op in ((hi, part_max, ALU.max), (lo, part_min, ALU.min)):
+                    nc.vector.tensor_tensor(
+                        out=(
+                            last[:].rearrange("p (r c) -> p r c", c=C)[:, cells, :]
+                            if width == C
+                            else extreme[:, cells, :width]
+                        ),
+                        in0=extreme[:, cells, :width],
+                        in1=extreme[:, cells, width : 2 * width],
+                        op=op,
+                    )
 
         flipped = psum.tile([P, 2, P], BF16, tag="flip")
         nc.tensor.transpose(flipped[:, 0, :], part_max[:], ident_bf16[:])
@@ -148,8 +156,22 @@ def tile_shapeletencoder_pa_k_kernel(tc, x, W0, b0, W1, b1, out):
         out_acc = psum.tile([P, K1], F32)
         acc = []
 
+        closing_round = {W1_PAIRS + (c + 1) * (PASSES // 2) + 1: c for c in range(C)}
         regrouped = []
-        for i in range(PAIRS + 1):
+        for i in range(PAIRS + 2):
+            closing = closing_round.get(i)
+
+            if closing is not None:
+                own_columns = h0_grouped[:, closing].rearrange("p (r k) t -> p r k t", k=C)
+                for t in range(FILTER_TILES):
+                    nc.scalar.activation(
+                        out=own_columns[:, :, closing, t],
+                        in_=acc[t][:].rearrange("p (r k) -> p r k", k=C)[:, :, closing],
+                        func=ACT.Relu,
+                        bias=b0_cols[:, FILTER_TILES * closing + t : FILTER_TILES * closing + t + 1],
+                        scale=1.0,
+                    )
+
             fresh = []
             if i < PAIRS:
                 for h in range(2):
@@ -170,7 +192,6 @@ def tile_shapeletencoder_pa_k_kernel(tc, x, W0, b0, W1, b1, out):
                         out=w1_codes[:, number, :].bitcast(FP8X4), scales=w1_scales[:, number, :], in_=values
                     )
                     continue
-
                 c, g = divmod(number - C, PASSES)
                 w0_codes = code_pool.tile([P, K0], U32, align_bytes=64)
                 w0_scales = code_pool.tile([P, K0], U8, align_bytes=64)
@@ -188,33 +209,23 @@ def tile_shapeletencoder_pa_k_kernel(tc, x, W0, b0, W1, b1, out):
                         start=(g == 0),
                         stop=(g == PASSES - 1),
                     )
-                if g < PASSES - 1:
-                    continue
+            regrouped = fresh
 
-                own_columns = h0_grouped[:, c].rearrange("p (r k) t -> p r k t", k=C)
-                for t in range(FILTER_TILES):
-                    nc.scalar.activation(
-                        out=own_columns[:, :, c, t],
-                        in_=acc[t][:].rearrange("p (r k) -> p r k", k=C)[:, :, c],
-                        func=ACT.Relu,
-                        bias=b0_cols[:, FILTER_TILES * c + t : FILTER_TILES * c + t + 1],
-                        scale=1.0,
-                    )
+            if closing is not None:
                 nc.vector.quantize_mx(
-                    out=h0_codes[:, c, :].bitcast(FP8X4),
-                    scales=h0_scales[:, c, :],
-                    in_=h0_grouped[:, c].rearrange("p m t -> p (m t)"),
+                    out=h0_codes[:, closing, :].bitcast(FP8X4),
+                    scales=h0_scales[:, closing, :],
+                    in_=h0_grouped[:, closing].rearrange("p m t -> p (m t)"),
                 )
                 nc.tensor.matmul_mx(
                     out=out_acc[:],
-                    lhsT=h0_codes[:, c, :].bitcast(FP8X4),
-                    lhsT_scale=h0_scales[:, c, :],
-                    rhs=w1_codes[:, c, :].bitcast(FP8X4),
-                    rhs_scale=w1_scales[:, c, :],
-                    start=(c == 0),
-                    stop=(c == C - 1),
+                    lhsT=h0_codes[:, closing, :].bitcast(FP8X4),
+                    lhsT_scale=h0_scales[:, closing, :],
+                    rhs=w1_codes[:, closing, :].bitcast(FP8X4),
+                    rhs_scale=w1_scales[:, closing, :],
+                    start=(closing == 0),
+                    stop=(closing == C - 1),
                 )
-            regrouped = fresh
 
         result = keep.tile([P, K1], F32)
         out_rows = out.rearrange("b s c k -> (b s c) k")

@@ -27,6 +27,7 @@ HEAD_PAIRS = 5
 RAW_BUFS = 10
 GROUPED_BUFS = 12
 CODE_BUFS = 8
+RUN = 8
 X_ROUND = 4
 
 
@@ -178,8 +179,8 @@ def tile_shapeletencoder_pa_k_kernel(tc, x, W0, b0, W1, b1, out):
                     grouped = grouped_pool.tile([P, K0, PACK], BF16, align_bytes=64)
                     copy = nc.vector.tensor_copy if (h == 1 and i >= HEAD_PAIRS) else nc.scalar.copy
                     copy(
-                        out=grouped[:].rearrange("p (w i) t -> p w t i", i=4),
-                        in_=raws[i][:, h].rearrange("p t (w i) -> p w t i", i=4),
+                        out=grouped[:].rearrange("p (w i) t -> p w t i", i=RUN),
+                        in_=raws[i][:, h].rearrange("p t (w i) -> p w t i", i=RUN),
                     )
                     fresh.append((2 * i + h, grouped))
                 if i + RAW_BUFS < PAIRS:

@@ -119,7 +119,7 @@ def tile_shapeletencoder_pa_k_kernel(tc, x, W0, b0, W1, b1, out):
         nc.vector.tensor_scalar(out=mid_repeated[:], in0=halves[:], scalar1=total[:, 0:1], scalar2=None, op0=ALU.mult)
         mid = psum.tile([P, P], F32)
         nc.tensor.transpose(mid[:], mid_repeated[:], ident_f32[:])
-        mid_rjc = mid[:].rearrange("p (r c) -> p r c", c=C).unsqueeze(2).to_broadcast([P, R, PACK, C])
+        mid_rcj = mid[:].rearrange("p (r c) -> p r c", c=C).unsqueeze(3).to_broadcast([P, R, C, PACK])
 
         x_codes = keep.tile([P, PASSES, P], U32, align_bytes=64)
         x_scales = keep.tile([P, PASSES, P], U8, align_bytes=64)
@@ -132,9 +132,9 @@ def tile_shapeletencoder_pa_k_kernel(tc, x, W0, b0, W1, b1, out):
                 for k in range(X_ROUND):
                     first = (X_ROUND * q + k) * PACK * C
                     nc.vector.tensor_tensor(
-                        out=n_grouped[:, k, :].rearrange("p (r c j) -> p r j c", r=R, c=C, j=PACK),
-                        in0=x_sb[:, :, first : first + PACK * C].rearrange("p r (j c) -> p r j c", c=C),
-                        in1=mid_rjc,
+                        out=n_grouped[:, k, :].rearrange("p (r c j) -> p r c j", r=R, c=C, j=PACK),
+                        in0=x_sb[:, :, first : first + PACK * C].rearrange("p r (j c) -> p r c j", c=C),
+                        in1=mid_rcj,
                         op=ALU.subtract,
                     )
             if q > 0:

@@ -23,7 +23,9 @@ FLOPS = 2 * R * C * (L * K0 + K0 * K1)
 
 W1_PAIRS = C // 2
 PAIRS = W1_PAIRS + C * PASSES // 2
-HEAD_PAIRS = 5
+HEAD_PAIRS = 8
+GPSIMD_PASSES = (8, 9, 10)
+GPSIMD_PARTS = 2
 RAW_BUFS = 10
 GROUPED_BUFS = 12
 CODE_BUFS = 8
@@ -52,33 +54,61 @@ def tile_shapeletencoder_pa_k_kernel(tc, x, W0, b0, W1, b1, out):
         h0_grouped = keep.tile([P, C, P, PACK], BF16, align_bytes=64)
         nc.vector.memset(h0_grouped[:], 0.0)
 
+        w0_rows = W0.rearrange("c (p g j) f -> c p g j f", p=P, g=PASSES, j=PACK)
+        w1_rows = W1.rearrange("c (t p) n -> p c t n", p=P)
         x_sb = keep.tile([P, R, OWN * C], BF16)
-        for b in range(B):
+
+        def load_x(b):
             nc.sync.dma_start(
                 out=x_sb[:, S * b : S * (b + 1), :],
                 in_=x[b].rearrange("(s p f) c -> p s (f c)", s=S, p=P, f=OWN),
             )
 
-        nc.sync.dma_start(out=b0_rows[0 : C * FILTER_TILES, :], in_=b0.rearrange("c (t p) -> (c t) p", p=P))
-
-        w0_rows = W0.rearrange("c (p g j) f -> c p g j f", p=P, g=PASSES, j=PACK)
-        w1_rows = W1.rearrange("c (t p) n -> p c t n", p=P)
-
         def load_pair(i):
             raw = raw_pool.tile([P, 2, PACK, K0], BF16, name="raw")
-            if i < W1_PAIRS:
-                rows = w1_rows[:, 2 * i : 2 * i + 2]
-            else:
-                c, g = divmod(2 * (i - W1_PAIRS), PASSES)
-                rows = w0_rows[c, :, g : g + 2]
-            nc.sync.dma_start(out=raw[:], in_=rows)
+            c, g = divmod(2 * (i - W1_PAIRS), PASSES)
+            nc.sync.dma_start(out=raw[:], in_=w0_rows[c, :, g : g + 2])
             return raw
 
-        raws = [load_pair(i) for i in range(RAW_BUFS)]
+        raws = []
+        for i in range(W1_PAIRS):
+            raw = raw_pool.tile([P, 2, PACK, K0], BF16, name="raw")
+            raws.append(raw)
+        nc.sync.dma_start(out=raws[0][:, 0], in_=w1_rows[:, 0])
+        load_x(0)
+        load_x(1)
+        nc.sync.dma_start(out=raws[0][:, 1], in_=w1_rows[:, 1])
+        load_x(2)
+        nc.sync.dma_start(out=raws[1][:, 0], in_=w1_rows[:, 2])
+        load_x(3)
+        nc.sync.dma_start(out=raws[1][:, 1], in_=w1_rows[:, 3])
+
+        nc.sync.dma_start(out=b0_rows[0 : C * FILTER_TILES, :], in_=b0.rearrange("c (t p) -> (c t) p", p=P))
+        raws.extend([load_pair(i) for i in range(W1_PAIRS, RAW_BUFS)])
 
         b1_rows = keep.tile([P, K1], BF16)
         for c in range(C):
             nc.sync.dma_start(out=b1_rows[c:P:C, :], in_=b1[c].partition_broadcast(R))
+
+        def regroup(number, copy):
+            grouped = grouped_pool.tile([P, K0, PACK], BF16, align_bytes=64, name="grouped")
+            copy(
+                out=grouped[:].rearrange("p (w i) t -> p w t i", i=RUN),
+                in_=raws[number // 2][:, number % 2].rearrange("p t (w i) -> p w t i", i=RUN),
+            )
+            return grouped
+
+        w1_codes = keep.tile([P, C, K1], U32, align_bytes=64)
+        w1_scales = keep.tile([P, C, K1], U8, align_bytes=64)
+        w1_grouped = [regroup(c, nc.scalar.copy) for c in range(C)]
+        raws.extend([load_pair(i) for i in range(RAW_BUFS, RAW_BUFS + W1_PAIRS)])
+
+        def quantise_w1(c):
+            nc.vector.quantize_mx(
+                out=w1_codes[:, c, :].bitcast(FP8X4),
+                scales=w1_scales[:, c, :],
+                in_=w1_grouped[c][:].rearrange("p w t -> p (w t)"),
+            )
 
         hi = keep.tile([P, R, OWN * C // 2], BF16)
         lo = keep.tile([P, R, OWN * C // 2], BF16)
@@ -110,6 +140,8 @@ def tile_shapeletencoder_pa_k_kernel(tc, x, W0, b0, W1, b1, out):
         flipped = psum.tile([P, 2, P], BF16, tag="flip")
         nc.tensor.transpose(flipped[:, 0, :], part_max[:], ident_bf16[:])
         nc.tensor.transpose(flipped[:, 1, :], part_min[:], ident_bf16[:])
+        quantise_w1(0)
+        quantise_w1(1)
         ends = keep.tile([P, 2], F32)
         nc.vector.tensor_reduce(out=ends[:, 0:1], in_=flipped[:, 0, :], axis=mybir.AxisListType.X, op=ALU.max)
         nc.vector.tensor_reduce(out=ends[:, 1:2], in_=flipped[:, 1, :], axis=mybir.AxisListType.X, op=ALU.min)
@@ -119,6 +151,24 @@ def tile_shapeletencoder_pa_k_kernel(tc, x, W0, b0, W1, b1, out):
         nc.vector.tensor_scalar(out=mid_repeated[:], in0=halves[:], scalar1=total[:, 0:1], scalar2=None, op0=ALU.mult)
         mid = psum.tile([P, P], F32)
         nc.tensor.transpose(mid[:], mid_repeated[:], ident_f32[:])
+        quantise_w1(2)
+        quantise_w1(3)
+        one = keep.tile([P, 1], F32)
+        nc.vector.memset(one[:], 1.0)
+        gpsimd_grouped = {}
+        for number in GPSIMD_PASSES:
+            grouped = keep.tile([P, K0, PACK], BF16, align_bytes=64, name="gpsimd_grouped", bufs=len(GPSIMD_PASSES))
+            gpsimd_grouped[number] = grouped
+            for part in range(GPSIMD_PARTS):
+                cols = slice(K0 // GPSIMD_PARTS * part, K0 // GPSIMD_PARTS * (part + 1))
+                nc.gpsimd.tensor_scalar(
+                    out=grouped[:, cols, :],
+                    in0=raws[number // 2][:, number % 2, :, cols].rearrange("p t w -> p w t"),
+                    scalar1=one[:, 0:1],
+                    scalar2=0.0,
+                    op0=ALU.mult,
+                    op1=ALU.add,
+                )
         mid_rcj = mid[:].rearrange("p (r c) -> p r c", c=C).unsqueeze(3).to_broadcast([P, R, C, PACK])
 
         x_codes = keep.tile([P, PASSES, P], U32, align_bytes=64)
@@ -150,8 +200,6 @@ def tile_shapeletencoder_pa_k_kernel(tc, x, W0, b0, W1, b1, out):
         b0_cols = keep.tile([P, C * FILTER_TILES], F32)
         nc.vector.tensor_copy(out=b0_cols[:], in_=b0_flipped[:, 0 : C * FILTER_TILES])
 
-        w1_codes = keep.tile([P, C, K1], U32, align_bytes=64)
-        w1_scales = keep.tile([P, C, K1], U8, align_bytes=64)
         h0_codes = keep.tile([P, C, P], U32, align_bytes=64)
         h0_scales = keep.tile([P, C, P], U8, align_bytes=64)
         out_acc = psum.tile([P, K1], F32)
@@ -159,7 +207,7 @@ def tile_shapeletencoder_pa_k_kernel(tc, x, W0, b0, W1, b1, out):
 
         closing_round = {W1_PAIRS + (c + 1) * (PASSES // 2) + 1: c for c in range(C)}
         regrouped = []
-        for i in range(PAIRS + 2):
+        for i in range(W1_PAIRS, PAIRS + 2):
             closing = closing_round.get(i)
 
             if closing is not None:
@@ -176,23 +224,15 @@ def tile_shapeletencoder_pa_k_kernel(tc, x, W0, b0, W1, b1, out):
             fresh = []
             if i < PAIRS:
                 for h in range(2):
-                    grouped = grouped_pool.tile([P, K0, PACK], BF16, align_bytes=64)
+                    number = 2 * i + h
                     copy = nc.vector.tensor_copy if (h == 1 and i >= HEAD_PAIRS) else nc.scalar.copy
-                    copy(
-                        out=grouped[:].rearrange("p (w i) t -> p w t i", i=RUN),
-                        in_=raws[i][:, h].rearrange("p t (w i) -> p w t i", i=RUN),
-                    )
-                    fresh.append((2 * i + h, grouped))
-                if i + RAW_BUFS < PAIRS:
-                    raws.append(load_pair(i + RAW_BUFS))
+                    grouped = gpsimd_grouped[number] if number in GPSIMD_PASSES else regroup(number, copy)
+                    fresh.append((number, grouped))
+                if len(raws) < PAIRS:
+                    raws.append(load_pair(len(raws)))
 
             for number, grouped in regrouped:
                 values = grouped[:].rearrange("p w t -> p (w t)")
-                if number < C:
-                    nc.vector.quantize_mx(
-                        out=w1_codes[:, number, :].bitcast(FP8X4), scales=w1_scales[:, number, :], in_=values
-                    )
-                    continue
                 c, g = divmod(number - C, PASSES)
                 w0_codes = code_pool.tile([P, K0], U32, align_bytes=64)
                 w0_scales = code_pool.tile([P, K0], U8, align_bytes=64)

@@ -26,11 +26,11 @@ PAIRS = W1_PAIRS + C * PASSES // 2
 HEAD_PAIRS = 8
 GPSIMD_PASSES = (8, 9, 10)
 GPSIMD_PARTS = 2
-RAW_BUFS = 10
+RAW_BUFS = 9
 GROUPED_BUFS = 12
 CODE_BUFS = 8
 RUN = 8
-X_ROUND = 4
+X_ROUND = 8
 
 
 def tile_shapeletencoder_pa_k_kernel(tc, x, W0, b0, W1, b1, out):
@@ -173,27 +173,25 @@ def tile_shapeletencoder_pa_k_kernel(tc, x, W0, b0, W1, b1, out):
 
         x_codes = keep.tile([P, PASSES, P], U32, align_bytes=64)
         x_scales = keep.tile([P, PASSES, P], U8, align_bytes=64)
-        x_rounds = PASSES // X_ROUND
         n_tiles = []
-        for q in range(x_rounds + 1):
-            if q < x_rounds:
-                n_grouped = keep.tile([P, X_ROUND, P * PACK], BF16, bufs=2, align_bytes=64)
-                n_tiles.append(n_grouped)
-                for k in range(X_ROUND):
-                    first = (X_ROUND * q + k) * PACK * C
-                    nc.vector.tensor_tensor(
-                        out=n_grouped[:, k, :].rearrange("p (r c j) -> p r c j", r=R, c=C, j=PACK),
-                        in0=x_sb[:, :, first : first + PACK * C].rearrange("p r (j c) -> p r c j", c=C),
-                        in1=mid_rcj,
-                        op=ALU.subtract,
-                    )
-            if q > 0:
-                done = slice(X_ROUND * (q - 1), X_ROUND * q)
-                nc.vector.quantize_mx(
-                    out=x_codes[:, done, :].rearrange("p g m -> p (g m)").bitcast(FP8X4),
-                    scales=x_scales[:, done, :].rearrange("p g m -> p (g m)"),
-                    in_=n_tiles[q - 1][:].rearrange("p g w -> p (g w)"),
+        for q in range(PASSES // X_ROUND):
+            n_grouped = keep.tile([P, X_ROUND, P * PACK], BF16, bufs=PASSES // X_ROUND, align_bytes=64)
+            n_tiles.append(n_grouped)
+            for k in range(X_ROUND):
+                first = (X_ROUND * q + k) * PACK * C
+                nc.vector.tensor_tensor(
+                    out=n_grouped[:, k, :].rearrange("p (r c j) -> p r c j", r=R, c=C, j=PACK),
+                    in0=x_sb[:, :, first : first + PACK * C].rearrange("p r (j c) -> p r c j", c=C),
+                    in1=mid_rcj,
+                    op=ALU.subtract,
                 )
+        for q in range(PASSES // X_ROUND):
+            done = slice(X_ROUND * q, X_ROUND * (q + 1))
+            nc.vector.quantize_mx(
+                out=x_codes[:, done, :].rearrange("p g m -> p (g m)").bitcast(FP8X4),
+                scales=x_scales[:, done, :].rearrange("p g m -> p (g m)"),
+                in_=n_tiles[q][:].rearrange("p g w -> p (g w)"),
+            )
 
         b0_flipped = psum.tile([P, P], BF16, tag="flip")
         nc.tensor.transpose(b0_flipped[:], b0_rows[:], ident_bf16[:])

@@ -24,12 +24,14 @@ FLOPS = 2 * R * C * (L * K0 + K0 * K1)
 W1_PAIRS = C // 2
 PAIRS = W1_PAIRS + C * PASSES // 2
 HEAD_PAIRS = 8
+SCALAR_EXTRA = 9
 GPSIMD_PASSES = (8, 9, 10)
 GPSIMD_PARTS = 2
 RAW_BUFS = 9
-GROUPED_BUFS = 12
-CODE_BUFS = 8
+GROUPED_BUFS = 7
+CODE_BUFS = 4
 RUN = 8
+LEAD = 3
 X_ROUND = 8
 
 
@@ -90,28 +92,36 @@ def tile_shapeletencoder_pa_k_kernel(tc, x, W0, b0, W1, b1, out):
         for c in range(C):
             nc.sync.dma_start(out=b1_rows[c:P:C, :], in_=b1[c].partition_broadcast(R))
 
-        def regroup(number, copy):
-            grouped = grouped_pool.tile([P, K0, PACK], BF16, align_bytes=64, name="grouped")
+        def scalar_alone(i):
+            return i < HEAD_PAIRS or (i - HEAD_PAIRS) % SCALAR_EXTRA == SCALAR_EXTRA - 1
+
+        def grouped_tile():
+            grouped = grouped_pool.tile([P, 2, K0, PACK], BF16, align_bytes=64, name="grouped")
+            return grouped
+
+        def regroup(grouped, number, copy):
             copy(
-                out=grouped[:].rearrange("p (w i) t -> p w t i", i=RUN),
+                out=grouped[:, number % 2].rearrange("p (w i) t -> p w t i", i=RUN),
                 in_=raws[number // 2][:, number % 2].rearrange("p t (w i) -> p w t i", i=RUN),
             )
-            return grouped
 
         w1_codes = keep.tile([P, C, K1], U32, align_bytes=64)
         w1_scales = keep.tile([P, C, K1], U8, align_bytes=64)
-        w1_grouped = [regroup(c, nc.scalar.copy) for c in range(C)]
+        w1_grouped = [grouped_tile() for i in range(W1_PAIRS)]
+        for c in range(C):
+            regroup(w1_grouped[c // 2], c, nc.scalar.copy)
         raws.extend([load_pair(i) for i in range(RAW_BUFS, RAW_BUFS + W1_PAIRS)])
 
-        def quantise_w1(c):
+        def quantise_w1(i):
+            both = slice(2 * i, 2 * i + 2)
             nc.vector.quantize_mx(
-                out=w1_codes[:, c, :].bitcast(FP8X4),
-                scales=w1_scales[:, c, :],
-                in_=w1_grouped[c][:].rearrange("p w t -> p (w t)"),
+                out=w1_codes[:, both, :].rearrange("p h w -> p (h w)").bitcast(FP8X4),
+                scales=w1_scales[:, both, :].rearrange("p h w -> p (h w)"),
+                in_=w1_grouped[i][:].rearrange("p h w t -> p (h w t)"),
             )
 
-        hi = keep.tile([P, R, OWN * C // 2], BF16)
-        lo = keep.tile([P, R, OWN * C // 2], BF16)
+        hi = keep.tile([P, R, OWN * C // 2], BF16, tag="x_work", bufs=2, align_bytes=64)
+        lo = keep.tile([P, R, OWN * C // 2], BF16, tag="x_work", bufs=2, align_bytes=64)
         part_max = keep.tile([P, R * C], BF16)
         part_min = keep.tile([P, R * C], BF16)
         for first_b in range(0, B, 2):
@@ -141,7 +151,6 @@ def tile_shapeletencoder_pa_k_kernel(tc, x, W0, b0, W1, b1, out):
         nc.tensor.transpose(flipped[:, 0, :], part_max[:], ident_bf16[:])
         nc.tensor.transpose(flipped[:, 1, :], part_min[:], ident_bf16[:])
         quantise_w1(0)
-        quantise_w1(1)
         ends = keep.tile([P, 2], F32)
         nc.vector.tensor_reduce(out=ends[:, 0:1], in_=flipped[:, 0, :], axis=mybir.AxisListType.X, op=ALU.max)
         nc.vector.tensor_reduce(out=ends[:, 1:2], in_=flipped[:, 1, :], axis=mybir.AxisListType.X, op=ALU.min)
@@ -151,18 +160,18 @@ def tile_shapeletencoder_pa_k_kernel(tc, x, W0, b0, W1, b1, out):
         nc.vector.tensor_scalar(out=mid_repeated[:], in0=halves[:], scalar1=total[:, 0:1], scalar2=None, op0=ALU.mult)
         mid = psum.tile([P, P], F32)
         nc.tensor.transpose(mid[:], mid_repeated[:], ident_f32[:])
-        quantise_w1(2)
-        quantise_w1(3)
+        quantise_w1(1)
         one = keep.tile([P, 1], F32)
         nc.vector.memset(one[:], 1.0)
         gpsimd_grouped = {}
         for number in GPSIMD_PASSES:
-            grouped = keep.tile([P, K0, PACK], BF16, align_bytes=64, name="gpsimd_grouped", bufs=len(GPSIMD_PASSES))
-            gpsimd_grouped[number] = grouped
+            if number // 2 not in gpsimd_grouped:
+                grouped = keep.tile([P, 2, K0, PACK], BF16, align_bytes=64, name="gpsimd_grouped", bufs=2)
+                gpsimd_grouped[number // 2] = grouped
             for part in range(GPSIMD_PARTS):
                 cols = slice(K0 // GPSIMD_PARTS * part, K0 // GPSIMD_PARTS * (part + 1))
                 nc.gpsimd.tensor_scalar(
-                    out=grouped[:, cols, :],
+                    out=gpsimd_grouped[number // 2][:, number % 2, cols, :],
                     in0=raws[number // 2][:, number % 2, :, cols].rearrange("p t w -> p w t"),
                     scalar1=one[:, 0:1],
                     scalar2=0.0,
@@ -175,7 +184,7 @@ def tile_shapeletencoder_pa_k_kernel(tc, x, W0, b0, W1, b1, out):
         x_scales = keep.tile([P, PASSES, P], U8, align_bytes=64)
         n_tiles = []
         for q in range(PASSES // X_ROUND):
-            n_grouped = keep.tile([P, X_ROUND, P * PACK], BF16, bufs=PASSES // X_ROUND, align_bytes=64)
+            n_grouped = keep.tile([P, X_ROUND, P * PACK], BF16, tag="x_work", bufs=2, align_bytes=64)
             n_tiles.append(n_grouped)
             for k in range(X_ROUND):
                 first = (X_ROUND * q + k) * PACK * C
@@ -204,7 +213,18 @@ def tile_shapeletencoder_pa_k_kernel(tc, x, W0, b0, W1, b1, out):
         acc = []
 
         closing_round = {W1_PAIRS + (c + 1) * (PASSES // 2) + 1: c for c in range(C)}
-        regrouped = []
+        second_layer_round = {i if c == C - 1 else i + LEAD: c for i, c in closing_round.items()}
+        regrouped = None
+        grouped_pairs = {}
+
+        def regroup_by_scalar(i):
+            grouped_pairs[i] = gpsimd_grouped[i] if i in gpsimd_grouped else grouped_tile()
+            for number in (2 * i, 2 * i + 1):
+                if number not in GPSIMD_PASSES and (number % 2 == 0 or scalar_alone(i)):
+                    regroup(grouped_pairs[i], number, nc.scalar.copy)
+
+        for i in range(W1_PAIRS, W1_PAIRS + LEAD):
+            regroup_by_scalar(i)
         for i in range(W1_PAIRS, PAIRS + 2):
             closing = closing_round.get(i)
 
@@ -219,37 +239,45 @@ def tile_shapeletencoder_pa_k_kernel(tc, x, W0, b0, W1, b1, out):
                         scale=1.0,
                     )
 
-            fresh = []
+            if i + LEAD < PAIRS:
+                regroup_by_scalar(i + LEAD)
+            fresh = None
             if i < PAIRS:
-                for h in range(2):
-                    number = 2 * i + h
-                    copy = nc.vector.tensor_copy if (h == 1 and i >= HEAD_PAIRS) else nc.scalar.copy
-                    grouped = gpsimd_grouped[number] if number in GPSIMD_PASSES else regroup(number, copy)
-                    fresh.append((number, grouped))
+                fresh = grouped_pairs[i]
+                if not scalar_alone(i):
+                    regroup(fresh, 2 * i + 1, nc.vector.tensor_copy)
                 if len(raws) < PAIRS:
                     raws.append(load_pair(len(raws)))
 
-            for number, grouped in regrouped:
-                values = grouped[:].rearrange("p w t -> p (w t)")
-                c, g = divmod(number - C, PASSES)
-                w0_codes = code_pool.tile([P, K0], U32, align_bytes=64)
-                w0_scales = code_pool.tile([P, K0], U8, align_bytes=64)
-                nc.vector.quantize_mx(out=w0_codes[:].bitcast(FP8X4), scales=w0_scales[:], in_=values)
-                if g == 0:
-                    acc = [psum.tile([P, P], F32, name="acc%d" % t) for t in range(FILTER_TILES)]
-                for t in range(FILTER_TILES):
-                    filters = slice(P * t, P * (t + 1))
-                    nc.tensor.matmul_mx(
-                        out=acc[t][:],
-                        lhsT=w0_codes[:, filters].bitcast(FP8X4),
-                        lhsT_scale=w0_scales[:, filters],
-                        rhs=x_codes[:, g, :].bitcast(FP8X4),
-                        rhs_scale=x_scales[:, g, :],
-                        start=(g == 0),
-                        stop=(g == PASSES - 1),
+            if regrouped is not None:
+                c, first_g = divmod(2 * (i - 1) - C, PASSES)
+                w0_codes = code_pool.tile([P, 2, K0], U32, align_bytes=64)
+                w0_scales = code_pool.tile([P, 2, K0], U8, align_bytes=64)
+                step = 1 if i == PAIRS else 2
+                for h in range(0, 2, step):
+                    nc.vector.quantize_mx(
+                        out=w0_codes[:, h : h + step].rearrange("p h w -> p (h w)").bitcast(FP8X4),
+                        scales=w0_scales[:, h : h + step].rearrange("p h w -> p (h w)"),
+                        in_=regrouped[:, h : h + step].rearrange("p h w t -> p (h w t)"),
                     )
+                if first_g == 0:
+                    acc = [psum.tile([P, P], F32, name="acc%d" % t) for t in range(FILTER_TILES)]
+                for h in range(2):
+                    for t in range(FILTER_TILES):
+                        filters = slice(P * t, P * (t + 1))
+                        g = first_g + h
+                        nc.tensor.matmul_mx(
+                            out=acc[t][:],
+                            lhsT=w0_codes[:, h, filters].bitcast(FP8X4),
+                            lhsT_scale=w0_scales[:, h, filters],
+                            rhs=x_codes[:, g, :].bitcast(FP8X4),
+                            rhs_scale=x_scales[:, g, :],
+                            start=(g == 0),
+                            stop=(g == PASSES - 1),
+                        )
             regrouped = fresh
 
+            closing = second_layer_round.get(i)
             if closing is not None:
                 nc.vector.quantize_mx(
                     out=h0_codes[:, closing, :].bitcast(FP8X4),

@@ -24,7 +24,7 @@ FLOPS = 2 * R * C * (L * K0 + K0 * K1)
 W1_PAIRS = C // 2
 PAIRS = W1_PAIRS + C * PASSES // 2
 HEAD_PAIRS = 8
-SCALAR_EXTRA = 9
+SCALAR_EXTRA = 14
 GPSIMD_PASSES = (8, 9, 10)
 GPSIMD_PARTS = 2
 RAW_BUFS = 9
@@ -87,10 +87,6 @@ def tile_shapeletencoder_pa_k_kernel(tc, x, W0, b0, W1, b1, out):
 
         nc.sync.dma_start(out=b0_rows[0 : C * FILTER_TILES, :], in_=b0.rearrange("c (t p) -> (c t) p", p=P))
         raws.extend([load_pair(i) for i in range(W1_PAIRS, RAW_BUFS)])
-
-        b1_rows = keep.tile([P, K1], BF16)
-        for c in range(C):
-            nc.sync.dma_start(out=b1_rows[c:P:C, :], in_=b1[c].partition_broadcast(R))
 
         def scalar_alone(i):
             return i < HEAD_PAIRS or (i - HEAD_PAIRS) % SCALAR_EXTRA == SCALAR_EXTRA - 1
@@ -251,30 +247,43 @@ def tile_shapeletencoder_pa_k_kernel(tc, x, W0, b0, W1, b1, out):
 
             if regrouped is not None:
                 c, first_g = divmod(2 * (i - 1) - C, PASSES)
-                w0_codes = code_pool.tile([P, 2, K0], U32, align_bytes=64)
-                w0_scales = code_pool.tile([P, 2, K0], U8, align_bytes=64)
-                step = 1 if i == PAIRS else 2
-                for h in range(0, 2, step):
-                    nc.vector.quantize_mx(
-                        out=w0_codes[:, h : h + step].rearrange("p h w -> p (h w)").bitcast(FP8X4),
-                        scales=w0_scales[:, h : h + step].rearrange("p h w -> p (h w)"),
-                        in_=regrouped[:, h : h + step].rearrange("p h w t -> p (h w t)"),
-                    )
+                w0_codes = code_pool.tile([P, 2 * K0], U32, align_bytes=64)
+                w0_scales = code_pool.tile([P, 2 * K0], U8, align_bytes=64)
                 if first_g == 0:
                     acc = [psum.tile([P, P], F32, name="acc%d" % t) for t in range(FILTER_TILES)]
-                for h in range(2):
+
+                def quantise(columns):
+                    nc.vector.quantize_mx(
+                        out=w0_codes[:, columns].bitcast(FP8X4),
+                        scales=w0_scales[:, columns],
+                        in_=regrouped[:].rearrange("p h w t -> p (h w t)")[:, PACK * columns.start : PACK * columns.stop],
+                    )
+
+                def multiply(h, t):
+                    filters = slice(K0 * h + P * t, K0 * h + P * (t + 1))
+                    g = first_g + h
+                    nc.tensor.matmul_mx(
+                        out=acc[t][:],
+                        lhsT=w0_codes[:, filters].bitcast(FP8X4),
+                        lhsT_scale=w0_scales[:, filters],
+                        rhs=x_codes[:, g, :].bitcast(FP8X4),
+                        rhs_scale=x_scales[:, g, :],
+                        start=(g == 0),
+                        stop=(g == PASSES - 1),
+                    )
+
+                if i < PAIRS:
+                    quantise(slice(0, 2 * K0))
+                    for h in range(2):
+                        for t in range(FILTER_TILES):
+                            multiply(h, t)
+                else:
+                    quantise(slice(0, K0))
                     for t in range(FILTER_TILES):
-                        filters = slice(P * t, P * (t + 1))
-                        g = first_g + h
-                        nc.tensor.matmul_mx(
-                            out=acc[t][:],
-                            lhsT=w0_codes[:, h, filters].bitcast(FP8X4),
-                            lhsT_scale=w0_scales[:, h, filters],
-                            rhs=x_codes[:, g, :].bitcast(FP8X4),
-                            rhs_scale=x_scales[:, g, :],
-                            start=(g == 0),
-                            stop=(g == PASSES - 1),
-                        )
+                        multiply(0, t)
+                    for t in range(FILTER_TILES):
+                        quantise(slice(K0 + P * t, K0 + P * (t + 1)))
+                        multiply(1, t)
             regrouped = fresh
 
             closing = second_layer_round.get(i)
@@ -294,10 +303,14 @@ def tile_shapeletencoder_pa_k_kernel(tc, x, W0, b0, W1, b1, out):
                     stop=(closing == C - 1),
                 )
 
+        b1_rows = keep.tile([P, K1], BF16)
+        for c in range(C):
+            nc.sync.dma_start(out=b1_rows[c:P:C, :], in_=b1[c].partition_broadcast(R))
         result = keep.tile([P, K1], F32)
         out_rows = out.rearrange("b s c k -> (b s c) k")
-        for half in range(2):
-            cols = slice(K1 // 2 * half, K1 // 2 * (half + 1))
+        halves_of_row = [slice(K1 // 2 * half, K1 // 2 * (half + 1)) for half in range(2)]
+        for cols in halves_of_row:
             nc.vector.tensor_tensor(out=result[:, cols], in0=out_acc[:, cols], in1=b1_rows[:, cols], op=ALU.add)
-            nc.scalar.activation(out=result[:, cols], in_=result[:, cols], func=ACT.Relu)
-            nc.sync.dma_start(out=out_rows[:, cols], in_=result[:, cols])
+        for cols, queue in zip(halves_of_row, (nc.sync, nc.scalar)):
+            nc.vector.tensor_scalar(out=result[:, cols], in0=result[:, cols], scalar1=0.0, scalar2=None, op0=ALU.max)
+            queue.dma_start(out=out_rows[:, cols], in_=result[:, cols])

from contextlib import ExitStack

import concourse.mybir as mybir
from concourse.masks import make_identity

FP8X4 = mybir.dt.float8_e4m3fn_x4
BF16 = mybir.dt.bfloat16
F32 = mybir.dt.float32
U32 = mybir.dt.uint32
U8 = mybir.dt.uint8
ALU = mybir.AluOpType
ACT = mybir.ActivationFunctionType

P = 128
PACK = 4
B, S, L, C, K0, K1 = 4, 8, 8192, 4, 512, 512
R = B * S
PASSES = L // (P * PACK)
OWN = L // P
FILTER_TILES = K0 // P

FLOPS = 2 * R * C * (L * K0 + K0 * K1)

W1_PAIRS = C // 2
PAIRS = W1_PAIRS + C * PASSES // 2
HEAD_PAIRS = 8
SCALAR_EXTRA = 14
GPSIMD_PASSES = (8, 9, 10)
GPSIMD_PARTS = 2
RAW_BUFS = 9
GROUPED_BUFS = 7
CODE_BUFS = 4
RUN = 8
LEAD = 3
X_ROUND = 8


def tile_shapeletencoder_pa_k_kernel(tc, x, W0, b0, W1, b1, out):
    nc = tc.nc
    with ExitStack() as ctx:
        keep = ctx.enter_context(tc.tile_pool(name="keep", bufs=1))
        raw_pool = ctx.enter_context(tc.tile_pool(name="raw", bufs=RAW_BUFS))
        grouped_pool = ctx.enter_context(tc.tile_pool(name="grouped", bufs=GROUPED_BUFS))
        code_pool = ctx.enter_context(tc.tile_pool(name="codes", bufs=CODE_BUFS))
        psum = ctx.enter_context(tc.psum_pool(name="psum", bufs=1))
        ctx.enter_context(tc.manual_schedule())

        ident_bf16 = keep.tile([P, P], BF16)
        make_identity(nc, ident_bf16[:])
        ident_f32 = keep.tile([P, P], F32)
        make_identity(nc, ident_f32[:])
        halves = keep.tile([P, P], F32)
        nc.vector.memset(halves[:], 0.5)
        b0_rows = keep.tile([P, P], BF16)
        nc.vector.memset(b0_rows[:], 0.0)
        h0_grouped = keep.tile([P, C, P, PACK], BF16, align_bytes=64)
        nc.vector.memset(h0_grouped[:], 0.0)

        w0_rows = W0.rearrange("c (p g j) f -> c p g j f", p=P, g=PASSES, j=PACK)
        w1_rows = W1.rearrange("c (t p) n -> p c t n", p=P)
        x_sb = keep.tile([P, R, OWN * C], BF16)

        def load_x(b):
            nc.sync.dma_start(
                out=x_sb[:, S * b : S * (b + 1), :],
                in_=x[b].rearrange("(s p f) c -> p s (f c)", s=S, p=P, f=OWN),
            )

        def load_pair(i):
            raw = raw_pool.tile([P, 2, PACK, K0], BF16, name="raw")
            c, g = divmod(2 * (i - W1_PAIRS), PASSES)
            nc.sync.dma_start(out=raw[:], in_=w0_rows[c, :, g : g + 2])
            return raw

        raws = []
        for i in range(W1_PAIRS):
            raw = raw_pool.tile([P, 2, PACK, K0], BF16, name="raw")
            raws.append(raw)
        nc.sync.dma_start(out=raws[0][:, 0], in_=w1_rows[:, 0])
        load_x(0)
        load_x(1)
        nc.sync.dma_start(out=raws[0][:, 1], in_=w1_rows[:, 1])
        load_x(2)
        nc.sync.dma_start(out=raws[1][:, 0], in_=w1_rows[:, 2])
        load_x(3)
        nc.sync.dma_start(out=raws[1][:, 1], in_=w1_rows[:, 3])

        nc.sync.dma_start(out=b0_rows[0 : C * FILTER_TILES, :], in_=b0.rearrange("c (t p) -> (c t) p", p=P))
        raws.extend([load_pair(i) for i in range(W1_PAIRS, RAW_BUFS)])

        def scalar_alone(i):
            return i < HEAD_PAIRS or (i - HEAD_PAIRS) % SCALAR_EXTRA == SCALAR_EXTRA - 1

        def grouped_tile():
            grouped = grouped_pool.tile([P, 2, K0, PACK], BF16, align_bytes=64, name="grouped")
            return grouped

        def regroup(grouped, number, copy):
            copy(
                out=grouped[:, number % 2].rearrange("p (w i) t -> p w t i", i=RUN),
                in_=raws[number // 2][:, number % 2].rearrange("p t (w i) -> p w t i", i=RUN),
            )

        w1_codes = keep.tile([P, C, K1], U32, align_bytes=64)
        w1_scales = keep.tile([P, C, K1], U8, align_bytes=64)
        w1_grouped = [grouped_tile() for i in range(W1_PAIRS)]
        for c in range(C):
            regroup(w1_grouped[c // 2], c, nc.scalar.copy)
        raws.extend([load_pair(i) for i in range(RAW_BUFS, RAW_BUFS + W1_PAIRS)])

        def quantise_w1(i):
            both = slice(2 * i, 2 * i + 2)
            nc.vector.quantize_mx(
                out=w1_codes[:, both, :].rearrange("p h w -> p (h w)").bitcast(FP8X4),
                scales=w1_scales[:, both, :].rearrange("p h w -> p (h w)"),
                in_=w1_grouped[i][:].rearrange("p h w t -> p (h w t)"),
            )

        hi = keep.tile([P, R, OWN * C // 2], BF16, tag="x_work", bufs=2, align_bytes=64)
        lo = keep.tile([P, R, OWN * C // 2], BF16, tag="x_work", bufs=2, align_bytes=64)
        part_max = keep.tile([P, R * C], BF16)
        part_min = keep.tile([P, R * C], BF16)
        for first_b in range(0, B, 2):
            width = OWN * C // 2
            for b in (first_b, first_b + 1):
                cells = slice(S * b, S * (b + 1))
                for extreme, op in ((hi, ALU.max), (lo, ALU.min)):
                    nc.vector.tensor_tensor(
                        out=extreme[:, cells, :], in0=x_sb[:, cells, :width], in1=x_sb[:, cells, width:], op=op
                    )
            cells = slice(S * first_b, S * (first_b + 2))
            while width > C:
                width //= 2
                for extreme, last, op in ((hi, part_max, ALU.max), (lo, part_min, ALU.min)):
                    nc.vector.tensor_tensor(
                        out=(
                            last[:].rearrange("p (r c) -> p r c", c=C)[:, cells, :]
                            if width == C
                            else extreme[:, cells, :width]
                        ),
                        in0=extreme[:, cells, :width],
                        in1=extreme[:, cells, width : 2 * width],
                        op=op,
                    )

        flipped = psum.tile([P, 2, P], BF16, tag="flip")
        nc.tensor.transpose(flipped[:, 0, :], part_max[:], ident_bf16[:])
        nc.tensor.transpose(flipped[:, 1, :], part_min[:], ident_bf16[:])
        quantise_w1(0)
        ends = keep.tile([P, 2], F32)
        nc.vector.tensor_reduce(out=ends[:, 0:1], in_=flipped[:, 0, :], axis=mybir.AxisListType.X, op=ALU.max)
        nc.vector.tensor_reduce(out=ends[:, 1:2], in_=flipped[:, 1, :], axis=mybir.AxisListType.X, op=ALU.min)
        total = keep.tile([P, 1], F32)
        nc.vector.tensor_tensor(out=total[:], in0=ends[:, 0:1], in1=ends[:, 1:2], op=ALU.add)
        mid_repeated = keep.tile([P, P], F32)
        nc.vector.tensor_scalar(out=mid_repeated[:], in0=halves[:], scalar1=total[:, 0:1], scalar2=None, op0=ALU.mult)
        mid = psum.tile([P, P], F32)
        nc.tensor.transpose(mid[:], mid_repeated[:], ident_f32[:])
        quantise_w1(1)
        one = keep.tile([P, 1], F32)
        nc.vector.memset(one[:], 1.0)
        gpsimd_grouped = {}
        for number in GPSIMD_PASSES:
            if number // 2 not in gpsimd_grouped:
                grouped = keep.tile([P, 2, K0, PACK], BF16, align_bytes=64, name="gpsimd_grouped", bufs=2)
                gpsimd_grouped[number // 2] = grouped
            for part in range(GPSIMD_PARTS):
                cols = slice(K0 // GPSIMD_PARTS * part, K0 // GPSIMD_PARTS * (part + 1))
                nc.gpsimd.tensor_scalar(
                    out=gpsimd_grouped[number // 2][:, number % 2, cols, :],
                    in0=raws[number // 2][:, number % 2, :, cols].rearrange("p t w -> p w t"),
                    scalar1=one[:, 0:1],
                    scalar2=0.0,
                    op0=ALU.mult,
                    op1=ALU.add,
                )
        mid_rcj = mid[:].rearrange("p (r c) -> p r c", c=C).unsqueeze(3).to_broadcast([P, R, C, PACK])

        x_codes = keep.tile([P, PASSES, P], U32, align_bytes=64)
        x_scales = keep.tile([P, PASSES, P], U8, align_bytes=64)
        n_tiles = []
        for q in range(PASSES // X_ROUND):
            n_grouped = keep.tile([P, X_ROUND, P * PACK], BF16, tag="x_work", bufs=2, align_bytes=64)
            n_tiles.append(n_grouped)
            for k in range(X_ROUND):
                first = (X_ROUND * q + k) * PACK * C
                nc.vector.tensor_tensor(
                    out=n_grouped[:, k, :].rearrange("p (r c j) -> p r c j", r=R, c=C, j=PACK),
                    in0=x_sb[:, :, first : first + PACK * C].rearrange("p r (j c) -> p r c j", c=C),
                    in1=mid_rcj,
                    op=ALU.subtract,
                )
        for q in range(PASSES // X_ROUND):
            done = slice(X_ROUND * q, X_ROUND * (q + 1))
            nc.vector.quantize_mx(
                out=x_codes[:, done, :].rearrange("p g m -> p (g m)").bitcast(FP8X4),
                scales=x_scales[:, done, :].rearrange("p g m -> p (g m)"),
                in_=n_tiles[q][:].rearrange("p g w -> p (g w)"),
            )

        b0_flipped = psum.tile([P, P], BF16, tag="flip")
        nc.tensor.transpose(b0_flipped[:], b0_rows[:], ident_bf16[:])
        b0_cols = keep.tile([P, C * FILTER_TILES], F32)
        nc.vector.tensor_copy(out=b0_cols[:], in_=b0_flipped[:, 0 : C * FILTER_TILES])

        h0_codes = keep.tile([P, C, P], U32, align_bytes=64)
        h0_scales = keep.tile([P, C, P], U8, align_bytes=64)
        out_acc = psum.tile([P, K1], F32)
        acc = []

        closing_round = {W1_PAIRS + (c + 1) * (PASSES // 2) + 1: c for c in range(C)}
        second_layer_round = {i if c == C - 1 else i + LEAD: c for i, c in closing_round.items()}
        regrouped = None
        grouped_pairs = {}

        def regroup_by_scalar(i):
            grouped_pairs[i] = gpsimd_grouped[i] if i in gpsimd_grouped else grouped_tile()
            for number in (2 * i, 2 * i + 1):
                if number not in GPSIMD_PASSES and (number % 2 == 0 or scalar_alone(i)):
                    regroup(grouped_pairs[i], number, nc.scalar.copy)

        for i in range(W1_PAIRS, W1_PAIRS + LEAD):
            regroup_by_scalar(i)
        for i in range(W1_PAIRS, PAIRS + 2):
            closing = closing_round.get(i)

            if closing is not None:
                own_columns = h0_grouped[:, closing].rearrange("p (r k) t -> p r k t", k=C)
                for t in range(FILTER_TILES):
                    nc.scalar.activation(
                        out=own_columns[:, :, closing, t],
                        in_=acc[t][:].rearrange("p (r k) -> p r k", k=C)[:, :, closing],
                        func=ACT.Relu,
                        bias=b0_cols[:, FILTER_TILES * closing + t : FILTER_TILES * closing + t + 1],
                        scale=1.0,
                    )

            if i + LEAD < PAIRS:
                regroup_by_scalar(i + LEAD)
            fresh = None
            if i < PAIRS:
                fresh = grouped_pairs[i]
                if not scalar_alone(i):
                    regroup(fresh, 2 * i + 1, nc.vector.tensor_copy)
                if len(raws) < PAIRS:
                    raws.append(load_pair(len(raws)))

            if regrouped is not None:
                c, first_g = divmod(2 * (i - 1) - C, PASSES)
                w0_codes = code_pool.tile([P, 2 * K0], U32, align_bytes=64)
                w0_scales = code_pool.tile([P, 2 * K0], U8, align_bytes=64)
                if first_g == 0:
                    acc = [psum.tile([P, P], F32, name="acc%d" % t) for t in range(FILTER_TILES)]

                def quantise(columns):
                    nc.vector.quantize_mx(
                        out=w0_codes[:, columns].bitcast(FP8X4),
                        scales=w0_scales[:, columns],
                        in_=regrouped[:].rearrange("p h w t -> p (h w t)")[:, PACK * columns.start : PACK * columns.stop],
                    )

                def multiply(h, t):
                    filters = slice(K0 * h + P * t, K0 * h + P * (t + 1))
                    g = first_g + h
                    nc.tensor.matmul_mx(
                        out=acc[t][:],
                        lhsT=w0_codes[:, filters].bitcast(FP8X4),
                        lhsT_scale=w0_scales[:, filters],
                        rhs=x_codes[:, g, :].bitcast(FP8X4),
                        rhs_scale=x_scales[:, g, :],
                        start=(g == 0),
                        stop=(g == PASSES - 1),
                    )

                if i < PAIRS:
                    quantise(slice(0, 2 * K0))
                    for h in range(2):
                        for t in range(FILTER_TILES):
                            multiply(h, t)
                else:
                    quantise(slice(0, K0))
                    for t in range(FILTER_TILES):
                        multiply(0, t)
                    for t in range(FILTER_TILES):
                        quantise(slice(K0 + P * t, K0 + P * (t + 1)))
                        multiply(1, t)
            regrouped = fresh

            closing = second_layer_round.get(i)
            if closing is not None:
                nc.vector.quantize_mx(
                    out=h0_codes[:, closing, :].bitcast(FP8X4),
                    scales=h0_scales[:, closing, :],
                    in_=h0_grouped[:, closing].rearrange("p m t -> p (m t)"),
                )
                nc.tensor.matmul_mx(
                    out=out_acc[:],
                    lhsT=h0_codes[:, closing, :].bitcast(FP8X4),
                    lhsT_scale=h0_scales[:, closing, :],
                    rhs=w1_codes[:, closing, :].bitcast(FP8X4),
                    rhs_scale=w1_scales[:, closing, :],
                    start=(closing == 0),
                    stop=(closing == C - 1),
                )

        b1_rows = keep.tile([P, K1], BF16)
        for c in range(C):
            nc.sync.dma_start(out=b1_rows[c:P:C, :], in_=b1[c].partition_broadcast(R))
        result = keep.tile([P, K1], F32)
        out_rows = out.rearrange("b s c k -> (b s c) k")
        halves_of_row = [slice(K1 // 2 * half, K1 // 2 * (half + 1)) for half in range(2)]
        for cols in halves_of_row:
            nc.vector.tensor_tensor(out=result[:, cols], in0=out_acc[:, cols], in1=b1_rows[:, cols], op=ALU.add)
        for cols, queue in zip(halves_of_row, (nc.sync, nc.scalar)):
            nc.vector.tensor_scalar(out=result[:, cols], in0=result[:, cols], scalar1=0.0, scalar2=None, op0=ALU.max)
            queue.dma_start(out=out_rows[:, cols], in_=result[:, cols])
